import numpy as np
import ml_dtypes


def mxq(x, axis, fmt="e4m3"):
    dtype, down = {"e4m3": (ml_dtypes.float8_e4m3fn, 7), "e5m2": (ml_dtypes.float8_e5m2, 14)}[fmt]
    v = np.moveaxis(np.asarray(x, np.float32).astype(ml_dtypes.bfloat16).astype(np.float64), axis, -1)
    blocks = v.reshape(v.shape[:-1] + (-1, 32))
    amax = np.abs(blocks).max(-1, keepdims=True)
    byte = np.maximum(np.where(amax > 0, np.frexp(amax)[1] - 1 + 127, 0) - down, 1)
    scale = np.exp2(byte - 127.0)
    codes = (blocks / scale).astype(np.float32).astype(dtype).astype(np.float64)
    return np.moveaxis((codes * scale).reshape(v.shape), -1, axis)


WIDE = False


def mx_kscale(k):
    if not WIDE:
        return np.ones(k)
    levels = np.array([10, -10, 5, -5, 0])
    a = np.random.permutation(np.resize(levels, k // 512 * 4)).reshape(k // 512, 4)
    idx = np.arange(k)
    return np.exp2(a[idx // 512, idx % 128 // 32])


BF16 = ml_dtypes.bfloat16


def bf(x):
    return np.asarray(x, np.float32).astype(BF16)


def f64(x):
    return np.asarray(x).astype(np.float64)


E2M1 = np.array([0.0, 0.5, 1.0, 1.5, 2.0, 3.0, 4.0, 6.0, -0.0, -0.5, -1.0, -1.5, -2.0, -3.0, -4.0, -6.0])


def pack_weight(w, fmt):
    k, n = w.shape
    w = f64(bf(w)).reshape(k // 32, 32, n)
    amax = np.abs(w).max(1)
    if fmt == "e4m3":
        byte = np.frexp(amax)[1] - 1 + 127 - 7
    else:
        mant, ex = np.frexp(amax / 6.0)
        byte = np.where(mant > 0.5, ex, ex - 1) + 127
    byte = np.clip(np.where(amax > 0, byte, 1), 1, 254)
    scaled = (w * np.exp2(127.0 - byte)[:, None, :]).reshape(k, n).astype(np.float32)
    by_word = np.ascontiguousarray(scaled.reshape(k // 512, 128, 4, n).transpose(0, 1, 3, 2))
    if fmt == "e4m3":
        words = by_word.astype(ml_dtypes.float8_e4m3fn).view(np.uint8)
    else:
        c = by_word.astype(ml_dtypes.float4_e2m1fn).view(np.uint8) & 0xF
        words = c[..., 0::2] | (c[..., 1::2] << 4)
    return np.ascontiguousarray(words), np.ascontiguousarray(byte.astype(np.uint8).reshape(k // 512, 16, n))


def unpack_weight(words, scales, fmt):
    g, p, n, _ = words.shape
    if fmt == "e4m3":
        vals = np.ascontiguousarray(words).view(ml_dtypes.float8_e4m3fn).astype(np.float64)
    else:
        nib = np.empty((g, p, n, 4), np.uint8)
        nib[..., 0::2] = words & 0xF
        nib[..., 1::2] = words >> 4
        vals = E2M1[nib]
    vals = vals * np.repeat(np.exp2(scales.astype(np.float64) - 127.0), 8, axis=1)[..., None]
    return vals.transpose(0, 1, 3, 2).reshape(g * 512, n)

def pack4(w):
    words, scales = pack_weight(w, "e2m1")
    return words.reshape(words.shape[0], 128, -1), scales


def unpack4(words, scales):
    return unpack_weight(words.reshape(words.shape[0], 128, -1, 2), scales, "e2m1")


B, D, H = 256, 512, 512
M_SCALE = 1.5


def setup_inputs():
    s, t = mx_kscale(D), mx_kscale(H)
    x = bf(np.random.standard_normal((B, D)) * s)
    h_prev = bf(np.random.standard_normal((B, H)) * t)
    c_prev = bf(np.random.standard_normal((B, H)))
    W_ih = np.random.standard_normal((2 * H, D)) * 0.7 / np.sqrt(D) / s[None, :]
    b_ih = bf(np.random.standard_normal(2 * H) * 0.2)
    W_hh = np.random.standard_normal((2 * H, H)) * 0.7 / np.sqrt(H) / t[None, :]
    b_hh = bf(np.random.standard_normal(2 * H) * 0.2)
    log_lambda = bf(np.log(np.random.uniform(0.05, 0.5, H)))
    z_bias = bf(np.random.standard_normal(H) * 0.2)
    m_bias = bf(np.random.standard_normal(H) * 0.2)
    W_ih_words, W_ih_scales = pack4(np.ascontiguousarray(W_ih.T))
    W_hh_words, W_hh_scales = pack4(np.ascontiguousarray(W_hh.T))
    return {'x': x,
            'h_prev': h_prev,
            'c_prev': c_prev,
            'W_ih_words': W_ih_words,
            'W_ih_scales': W_ih_scales,
            'b_ih': b_ih,
            'W_hh_words': W_hh_words,
            'W_hh_scales': W_hh_scales,
            'b_hh': b_hh,
            'log_lambda': log_lambda,
            'z_bias': z_bias,
            'm_bias': m_bias}


def reference(x, h_prev, c_prev, W_ih_words, W_ih_scales, b_ih, W_hh_words, W_hh_scales, b_hh, log_lambda, z_bias, m_bias):
    gates = ((mxq(f64(x), 1, 'e4m3') @ unpack4(W_ih_words, W_ih_scales)) + f64(b_ih)
             + (mxq(f64(h_prev), 1, 'e4m3') @ unpack4(W_hh_words, W_hh_scales)) + f64(b_hh))
    z_raw, m_raw = gates[:, :H], gates[:, H:]
    z_t = np.tanh(z_raw + f64(z_bias))
    M_t = M_SCALE * np.tanh(m_raw + f64(m_bias))
    A_base = -np.exp(f64(log_lambda))
    innov = z_t - M_t * (A_base * f64(c_prev))
    return z_t, M_t, innov

@@ -1,0 +1,157 @@
+from contextlib import ExitStack
+
+import concourse.mybir as mybir
+from concourse.masks import make_identity
+
+F32 = mybir.dt.float32
+BF16 = mybir.dt.bfloat16
+I32 = mybir.dt.int32
+U8 = mybir.dt.uint8
+U32 = mybir.dt.uint32
+FP8X4 = mybir.dt.float8_e4m3fn_x4
+FP4X4 = mybir.dt.float4_e2m1fn_x4
+ACT = mybir.ActivationFunctionType
+ALU = mybir.AluOpType
+
+P = 128
+B = 256
+K = 512
+H = 512
+TILES = B // P
+Z_HALF, M_HALF = 0, 1
+M_SCALE = 1.5
+
+FLOPS = 2 * B * (2 * H) * (2 * K)
+
+
+def tile_koslmcell_pa_s_kernel(
+    tc,
+    x,
+    h_prev,
+    c_prev,
+    W_ih_words,
+    W_ih_scales,
+    b_ih,
+    W_hh_words,
+    W_hh_scales,
+    b_hh,
+    log_lambda,
+    z_bias,
+    m_bias,
+    out_0,
+    out_1,
+    out_2,
+):
+    nc = tc.nc
+
+    def by_tile(dram):
+        return dram.rearrange("(p t) j -> p t j", t=TILES)
+
+    with ExitStack() as stack:
+        keep = stack.enter_context(tc.tile_pool(name="keep", bufs=1))
+        psum_flip = stack.enter_context(tc.psum_pool(name="psum_flip", bufs=1))
+        psum_spread = stack.enter_context(tc.psum_pool(name="psum_spread", bufs=1))
+        psum_gates = stack.enter_context(tc.psum_pool(name="psum_gates", bufs=3))
+        stack.enter_context(tc.manual_schedule())
+
+        vec_rows = keep.tile([P, 3 * H], BF16)
+        nc.vector.memset(vec_rows[:], 0.0)
+        w_planes = keep.tile([P, 2, 2 * H], U8, align_bytes=64)
+        nc.vector.memset(w_planes[:].rearrange("p o n -> p (o n)").bitcast(I32), 0)
+        ones = keep.tile([P, P], BF16)
+        nc.vector.memset(ones[:], 1.0)
+        ident = keep.tile([P, P], F32)
+        make_identity(nc, ident[:])
+
+        nc.scalar.dma_start(out=vec_rows[0:1, 0 : 2 * H], in_=b_ih.unsqueeze(0))
+        nc.scalar.dma_start(out=vec_rows[1:2, 0 : 2 * H], in_=b_hh.unsqueeze(0))
+        nc.scalar.dma_start(out=vec_rows[2:3, 0:H], in_=z_bias.unsqueeze(0))
+        nc.scalar.dma_start(out=vec_rows[2:3, H : 2 * H], in_=m_bias.unsqueeze(0))
+        x_sb = keep.tile([P, TILES, K], BF16)
+        h_sb = keep.tile([P, TILES, K], BF16)
+        nc.sync.dma_start(out=x_sb[:], in_=by_tile(x))
+        nc.sync.dma_start(out=h_sb[:], in_=by_tile(h_prev))
+        w_words = keep.tile([P, 2, 4 * H], U8, align_bytes=64)
+        for o, words in enumerate((W_ih_words, W_hh_words)):
+            nc.sync.dma_start(out=w_words[:, o, :].bitcast(I32), in_=words[0].bitcast(I32))
+        for o, scales in enumerate((W_ih_scales, W_hh_scales)):
+            for q in range(4):
+                nc.sync.dma_start(
+                    out=w_planes[32 * q : 32 * q + 4, o, :].bitcast(I32),
+                    in_=scales[0, 4 * q : 4 * q + 4, :].bitcast(I32),
+                )
+        nc.gpsimd.dma_start(out=vec_rows[0:1, 2 * H : 3 * H], in_=log_lambda.unsqueeze(0))
+        c_sb = keep.tile([P, TILES, H], BF16)
+        nc.gpsimd.dma_start(out=c_sb[:], in_=by_tile(c_prev))
+
+        table_warm = keep.tile([P, 1], F32)
+        nc.scalar.activation(out=table_warm[:], in_=ones[:, 0:1], func=ACT.Tanh)
+
+        bias = keep.tile([P, 2, H], F32)
+        for half in (M_HALF, Z_HALF):
+            bias_ps = psum_spread.tile([P, H], F32, name="bias_ps_%d" % half)
+            nc.tensor.matmul(
+                out=bias_ps[:], lhsT=ones[:], rhs=vec_rows[:, H * half : H * (half + 1)], start=True, stop=True
+            )
+            nc.scalar.copy(out=bias[:, half, :], in_=bias_ps[:])
+
+        act_codes = keep.tile([P, TILES, 2, P], U32, align_bytes=64)
+        act_planes = keep.tile([P, TILES, 2, P], U8, align_bytes=64)
+        grouped = []
+        for t in range(TILES):
+            flipped = psum_flip.tile([P, 4, P], F32, name="flipped_%d" % t)
+            for o, act_sb in enumerate((x_sb, h_sb)):
+                for u in range(2):
+                    nc.tensor.transpose(
+                        flipped[:, 2 * o + u, :], act_sb[:].bitcast(F32)[:, t, u : K // 2 : 2], ident[:]
+                    )
+            grouped_t = keep.tile([P, 2, P, 4], BF16, align_bytes=64, name="grouped_%d" % t)
+            grouped.append(grouped_t)
+            copy_out = nc.vector.tensor_copy if t == 0 else nc.scalar.copy
+            copy_out(out=grouped_t[:].bitcast(F32), in_=flipped[:].rearrange("p (o u) r -> p o r u", u=2))
+        for t in range(TILES):
+            nc.vector.quantize_mx(
+                out=act_codes[:, t, :, :].rearrange("p o r -> p (o r)").bitcast(FP8X4),
+                scales=act_planes[:, t, :, :].rearrange("p o r -> p (o r)"),
+                in_=grouped[t][:].rearrange("p o r j -> p (o r j)"),
+            )
+
+        lam_ps = psum_spread.tile([P, H], F32)
+        nc.tensor.matmul(out=lam_ps[:], lhsT=ones[:], rhs=vec_rows[:, 2 * H : 3 * H], start=True, stop=True)
+        lam = keep.tile([P, H], F32)
+        nc.scalar.activation(out=lam[:], in_=lam_ps[:], func=ACT.Exp)
+        lam_scaled = keep.tile([P, H], F32)
+        nc.scalar.mul(out=lam_scaled[:], in_=lam[:], mul=M_SCALE)
+        decay_c = keep.tile([P, TILES, H], F32)
+        for t in range(TILES):
+            nc.gpsimd.tensor_tensor(out=decay_c[:, t, :], in0=c_sb[:, t, :], in1=lam_scaled[:], op=ALU.mult)
+
+        tanh = {}
+        for t in range(TILES):
+            for half in (M_HALF, Z_HALF):
+                gates = psum_gates.tile([P, H], F32, tag="gates", name="gates_%d_%d" % (t, half))
+                for o in range(2):
+                    nc.tensor.matmul_mx(
+                        out=gates[:],
+                        lhsT=act_codes[:, t, o, :].bitcast(FP8X4),
+                        lhsT_scale=act_planes[:, t, o, :],
+                        rhs=w_words[:, o, 2 * H * half : 2 * H * (half + 1)].bitcast(FP4X4),
+                        rhs_scale=w_planes[:, o, H * half : H * (half + 1)],
+                        start=(o == 0),
+                        stop=(o == 1),
+                    )
+                biased = keep.tile([P, H], F32, name="biased_%d_%d" % (t, half))
+                nc.vector.tensor_tensor(out=biased[:], in0=gates[:], in1=bias[:, half, :], op=ALU.add)
+                tanh[t, half] = keep.tile([P, H], F32, name="tanh_%d_%d" % (t, half))
+                nc.scalar.activation(out=tanh[t, half][:], in_=biased[:], func=ACT.Tanh)
+            nc.sync.dma_start(out=by_tile(out_0)[:, t, :], in_=tanh[t, Z_HALF][:])
+
+        for t in range(TILES):
+            m_t = keep.tile([P, H], F32, name="m_t_%d" % t)
+            nc.scalar.mul(out=m_t[:], in_=tanh[t, M_HALF][:], mul=M_SCALE)
+            nc.sync.dma_start(out=by_tile(out_1)[:, t, :], in_=m_t[:])
+            fed_back = keep.tile([P, H], F32, name="fed_back_%d" % t)
+            nc.vector.tensor_tensor(out=fed_back[:], in0=tanh[t, M_HALF][:], in1=decay_c[:, t, :], op=ALU.mult)
+            innov = keep.tile([P, H], F32, name="innov_%d" % t)
+            nc.vector.tensor_tensor(out=innov[:], in0=tanh[t, Z_HALF][:], in1=fed_back[:], op=ALU.add)
+            nc.sync.dma_start(out=by_tile(out_2)[:, t, :], in_=innov[:])

@@ -49,9 +49,7 @@ def tile_koslmcell_pa_s_kernel(
 
     with ExitStack() as stack:
         keep = stack.enter_context(tc.tile_pool(name="keep", bufs=1))
-        psum_flip = stack.enter_context(tc.psum_pool(name="psum_flip", bufs=1))
-        psum_spread = stack.enter_context(tc.psum_pool(name="psum_spread", bufs=1))
-        psum_gates = stack.enter_context(tc.psum_pool(name="psum_gates", bufs=3))
+        psum = stack.enter_context(tc.psum_pool(name="psum", bufs=8))
         stack.enter_context(tc.manual_schedule())
 
         vec_rows = keep.tile([P, 3 * H], BF16)
@@ -63,23 +61,27 @@ def tile_koslmcell_pa_s_kernel(
         ident = keep.tile([P, P], F32)
         make_identity(nc, ident[:])
 
-        nc.scalar.dma_start(out=vec_rows[0:1, 0 : 2 * H], in_=b_ih.unsqueeze(0))
-        nc.scalar.dma_start(out=vec_rows[1:2, 0 : 2 * H], in_=b_hh.unsqueeze(0))
-        nc.scalar.dma_start(out=vec_rows[2:3, 0:H], in_=z_bias.unsqueeze(0))
-        nc.scalar.dma_start(out=vec_rows[2:3, H : 2 * H], in_=m_bias.unsqueeze(0))
+        nc.sync.dma_start(out=vec_rows[0:1, 0 : 2 * H], in_=b_ih.unsqueeze(0))
+        nc.sync.dma_start(out=vec_rows[1:2, 0 : 2 * H], in_=b_hh.unsqueeze(0))
+        nc.sync.dma_start(out=vec_rows[2:3, 0:H], in_=z_bias.unsqueeze(0))
+        nc.sync.dma_start(out=vec_rows[2:3, H : 2 * H], in_=m_bias.unsqueeze(0))
         x_sb = keep.tile([P, TILES, K], BF16)
         h_sb = keep.tile([P, TILES, K], BF16)
-        nc.sync.dma_start(out=x_sb[:], in_=by_tile(x))
-        nc.sync.dma_start(out=h_sb[:], in_=by_tile(h_prev))
-        w_words = keep.tile([P, 2, 4 * H], U8, align_bytes=64)
-        for o, words in enumerate((W_ih_words, W_hh_words)):
-            nc.sync.dma_start(out=w_words[:, o, :].bitcast(I32), in_=words[0].bitcast(I32))
-        for o, scales in enumerate((W_ih_scales, W_hh_scales)):
+        nc.scalar.dma_start(out=x_sb[:], in_=by_tile(x))
+        nc.scalar.dma_start(out=h_sb[:], in_=by_tile(h_prev))
+
+        def load_scale_rows(o, scales):
             for q in range(4):
                 nc.sync.dma_start(
                     out=w_planes[32 * q : 32 * q + 4, o, :].bitcast(I32),
                     in_=scales[0, 4 * q : 4 * q + 4, :].bitcast(I32),
                 )
+
+        w_words = keep.tile([P, 2, 4 * H], U8, align_bytes=64)
+        load_scale_rows(0, W_ih_scales)
+        nc.sync.dma_start(out=w_words[:, 0, :].bitcast(I32), in_=W_ih_words[0].bitcast(I32))
+        nc.sync.dma_start(out=w_words[:, 1, :].bitcast(I32), in_=W_hh_words[0].bitcast(I32))
+        load_scale_rows(1, W_hh_scales)
         nc.gpsimd.dma_start(out=vec_rows[0:1, 2 * H : 3 * H], in_=log_lambda.unsqueeze(0))
         c_sb = keep.tile([P, TILES, H], BF16)
         nc.gpsimd.dma_start(out=c_sb[:], in_=by_tile(c_prev))
@@ -87,71 +89,78 @@ def tile_koslmcell_pa_s_kernel(
         table_warm = keep.tile([P, 1], F32)
         nc.scalar.activation(out=table_warm[:], in_=ones[:, 0:1], func=ACT.Tanh)
 
+        grouped = keep.tile([P, 2, TILES, P, 4], BF16, align_bytes=64)
+        act_codes = keep.tile([P, 2, TILES, P], U32, align_bytes=64)
+        act_planes = keep.tile([P, 2, TILES, P], U8, align_bytes=64)
+        for o, act_sb in enumerate((x_sb, h_sb)):
+            for t in range(TILES):
+                flipped = psum.tile([P, 2, P], F32, tag="bank", name="flipped_%d_%d" % (o, t))
+                for u in range(2):
+                    nc.tensor.transpose(flipped[:, u, :], act_sb[:].bitcast(F32)[:, t, u : K // 2 : 2], ident[:])
+                copy_out = nc.scalar.copy if t == 0 else nc.vector.tensor_copy
+                copy_out(out=grouped[:, o, t, :, :].bitcast(F32), in_=flipped[:].rearrange("p u r -> p r u"))
+                nc.vector.quantize_mx(
+                    out=act_codes[:, o, t, :].bitcast(FP8X4),
+                    scales=act_planes[:, o, t, :],
+                    in_=grouped[:, o, t, :, :].rearrange("p r j -> p (r j)"),
+                )
+
         bias = keep.tile([P, 2, H], F32)
         for half in (M_HALF, Z_HALF):
-            bias_ps = psum_spread.tile([P, H], F32, name="bias_ps_%d" % half)
+            bias_ps = psum.tile([P, H], F32, tag="bank", name="bias_ps_%d" % half)
             nc.tensor.matmul(
                 out=bias_ps[:], lhsT=ones[:], rhs=vec_rows[:, H * half : H * (half + 1)], start=True, stop=True
             )
             nc.scalar.copy(out=bias[:, half, :], in_=bias_ps[:])
-
-        act_codes = keep.tile([P, TILES, 2, P], U32, align_bytes=64)
-        act_planes = keep.tile([P, TILES, 2, P], U8, align_bytes=64)
-        grouped = []
-        for t in range(TILES):
-            flipped = psum_flip.tile([P, 4, P], F32, name="flipped_%d" % t)
-            for o, act_sb in enumerate((x_sb, h_sb)):
-                for u in range(2):
-                    nc.tensor.transpose(
-                        flipped[:, 2 * o + u, :], act_sb[:].bitcast(F32)[:, t, u : K // 2 : 2], ident[:]
-                    )
-            grouped_t = keep.tile([P, 2, P, 4], BF16, align_bytes=64, name="grouped_%d" % t)
-            grouped.append(grouped_t)
-            copy_out = nc.vector.tensor_copy if t == 0 else nc.scalar.copy
-            copy_out(out=grouped_t[:].bitcast(F32), in_=flipped[:].rearrange("p (o u) r -> p o r u", u=2))
-        for t in range(TILES):
-            nc.vector.quantize_mx(
-                out=act_codes[:, t, :, :].rearrange("p o r -> p (o r)").bitcast(FP8X4),
-                scales=act_planes[:, t, :, :].rearrange("p o r -> p (o r)"),
-                in_=grouped[t][:].rearrange("p o r j -> p (o r j)"),
-            )
-
-        lam_ps = psum_spread.tile([P, H], F32)
+        lam_ps = psum.tile([P, H], F32, tag="bank")
         nc.tensor.matmul(out=lam_ps[:], lhsT=ones[:], rhs=vec_rows[:, 2 * H : 3 * H], start=True, stop=True)
         lam = keep.tile([P, H], F32)
         nc.scalar.activation(out=lam[:], in_=lam_ps[:], func=ACT.Exp)
-        lam_scaled = keep.tile([P, H], F32)
-        nc.scalar.mul(out=lam_scaled[:], in_=lam[:], mul=M_SCALE)
         decay_c = keep.tile([P, TILES, H], F32)
         for t in range(TILES):
-            nc.gpsimd.tensor_tensor(out=decay_c[:, t, :], in0=c_sb[:, t, :], in1=lam_scaled[:], op=ALU.mult)
+            nc.gpsimd.tensor_tensor(out=decay_c[:, t, :], in0=c_sb[:, t, :], in1=lam[:], op=ALU.mult)
 
         tanh = {}
-        for t in range(TILES):
-            for half in (M_HALF, Z_HALF):
-                gates = psum_gates.tile([P, H], F32, tag="gates", name="gates_%d_%d" % (t, half))
-                for o in range(2):
-                    nc.tensor.matmul_mx(
-                        out=gates[:],
-                        lhsT=act_codes[:, t, o, :].bitcast(FP8X4),
-                        lhsT_scale=act_planes[:, t, o, :],
-                        rhs=w_words[:, o, 2 * H * half : 2 * H * (half + 1)].bitcast(FP4X4),
-                        rhs_scale=w_planes[:, o, H * half : H * (half + 1)],
-                        start=(o == 0),
-                        stop=(o == 1),
-                    )
-                biased = keep.tile([P, H], F32, name="biased_%d_%d" % (t, half))
-                nc.vector.tensor_tensor(out=biased[:], in0=gates[:], in1=bias[:, half, :], op=ALU.add)
-                tanh[t, half] = keep.tile([P, H], F32, name="tanh_%d_%d" % (t, half))
-                nc.scalar.activation(out=tanh[t, half][:], in_=biased[:], func=ACT.Tanh)
-            nc.sync.dma_start(out=by_tile(out_0)[:, t, :], in_=tanh[t, Z_HALF][:])
+        fed_back = {}
+
+        def gate(t, half):
+            gates = psum.tile([P, H], F32, tag="bank", name="gates_%d_%d" % (t, half))
+            for o in range(2):
+                nc.tensor.matmul_mx(
+                    out=gates[:],
+                    lhsT=act_codes[:, o, t, :].bitcast(FP8X4),
+                    lhsT_scale=act_planes[:, o, t, :],
+                    rhs=w_words[:, o, 2 * H * half : 2 * H * (half + 1)].bitcast(FP4X4),
+                    rhs_scale=w_planes[:, o, H * half : H * (half + 1)],
+                    start=(o == 0),
+                    stop=(o == 1),
+                )
+            biased = keep.tile([P, H], F32, name="biased_%d_%d" % (t, half))
+            nc.vector.tensor_tensor(out=biased[:], in0=gates[:], in1=bias[:, half, :], op=ALU.add)
+            tanh[t, half] = keep.tile([P, H], F32, name="tanh_%d_%d" % (t, half))
+            nc.scalar.activation(out=tanh[t, half][:], in_=biased[:], func=ACT.Tanh)
+
+        def innovate(t):
+            innov = keep.tile([P, H], F32, name="innov_%d" % t)
+            nc.vector.tensor_tensor(out=innov[:], in0=tanh[t, Z_HALF][:], in1=fed_back[t][:], op=ALU.add)
+            nc.sync.dma_start(out=by_tile(out_2)[:, t, :], in_=innov[:])
 
         for t in range(TILES):
+            gate(t, M_HALF)
             m_t = keep.tile([P, H], F32, name="m_t_%d" % t)
             nc.scalar.mul(out=m_t[:], in_=tanh[t, M_HALF][:], mul=M_SCALE)
             nc.sync.dma_start(out=by_tile(out_1)[:, t, :], in_=m_t[:])
-            fed_back = keep.tile([P, H], F32, name="fed_back_%d" % t)
-            nc.vector.tensor_tensor(out=fed_back[:], in0=tanh[t, M_HALF][:], in1=decay_c[:, t, :], op=ALU.mult)
-            innov = keep.tile([P, H], F32, name="innov_%d" % t)
-            nc.vector.tensor_tensor(out=innov[:], in0=tanh[t, Z_HALF][:], in1=fed_back[:], op=ALU.add)
-            nc.sync.dma_start(out=by_tile(out_2)[:, t, :], in_=innov[:])
+            if t > 0:
+                innovate(t - 1)
+            gate(t, Z_HALF)
+            nc.sync.dma_start(out=by_tile(out_0)[:, t, :], in_=tanh[t, Z_HALF][:])
+            fed_back[t] = keep.tile([P, H], F32, name="fed_back_%d" % t)
+            nc.vector.scalar_tensor_tensor(
+                out=fed_back[t][:],
+                in0=tanh[t, M_HALF][:],
+                scalar=M_SCALE,
+                in1=decay_c[:, t, :],
+                op0=ALU.mult,
+                op1=ALU.mult,
+            )
+        innovate(TILES - 1)

@@ -105,6 +105,16 @@ def tile_koslmcell_pa_s_kernel(
                     in_=grouped[:, o, t, :, :].rearrange("p r j -> p (r j)"),
                 )
 
+        lam_ps = psum.tile([P, H], F32, tag="bank")
+        nc.tensor.matmul(out=lam_ps[:], lhsT=ones[:], rhs=vec_rows[:, 2 * H : 3 * H], start=True, stop=True)
+        lam = keep.tile([P, H], F32)
+        nc.scalar.activation(out=lam[:], in_=lam_ps[:], func=ACT.Exp)
+        decay_c = keep.tile([P, TILES, H], F32)
+        for t in range(TILES):
+            nc.vector.scalar_tensor_tensor(
+                out=decay_c[:, t, :], in0=c_sb[:, t, :], scalar=M_SCALE, in1=lam[:], op0=ALU.mult, op1=ALU.mult
+            )
+
         bias = keep.tile([P, 2, H], F32)
         for half in (M_HALF, Z_HALF):
             bias_ps = psum.tile([P, H], F32, tag="bank", name="bias_ps_%d" % half)
@@ -112,13 +122,6 @@ def tile_koslmcell_pa_s_kernel(
                 out=bias_ps[:], lhsT=ones[:], rhs=vec_rows[:, H * half : H * (half + 1)], start=True, stop=True
             )
             nc.scalar.copy(out=bias[:, half, :], in_=bias_ps[:])
-        lam_ps = psum.tile([P, H], F32, tag="bank")
-        nc.tensor.matmul(out=lam_ps[:], lhsT=ones[:], rhs=vec_rows[:, 2 * H : 3 * H], start=True, stop=True)
-        lam = keep.tile([P, H], F32)
-        nc.scalar.activation(out=lam[:], in_=lam_ps[:], func=ACT.Exp)
-        decay_c = keep.tile([P, TILES, H], F32)
-        for t in range(TILES):
-            nc.gpsimd.tensor_tensor(out=decay_c[:, t, :], in0=c_sb[:, t, :], in1=lam[:], op=ALU.mult)
 
         tanh = {}
         fed_back = {}
@@ -140,6 +143,15 @@ def tile_koslmcell_pa_s_kernel(
             tanh[t, half] = keep.tile([P, H], F32, name="tanh_%d_%d" % (t, half))
             nc.scalar.activation(out=tanh[t, half][:], in_=biased[:], func=ACT.Tanh)
 
+        def scale_m(t):
+            m_t = keep.tile([P, H], F32, name="m_t_%d" % t)
+            nc.scalar.mul(out=m_t[:], in_=tanh[t, M_HALF][:], mul=M_SCALE)
+            nc.sync.dma_start(out=by_tile(out_1)[:, t, :], in_=m_t[:])
+
+        def feed_back(t, engine):
+            fed_back[t] = keep.tile([P, H], F32, name="fed_back_%d" % t)
+            engine.tensor_tensor(out=fed_back[t][:], in0=tanh[t, M_HALF][:], in1=decay_c[:, t, :], op=ALU.mult)
+
         def innovate(t):
             innov = keep.tile([P, H], F32, name="innov_%d" % t)
             nc.vector.tensor_tensor(out=innov[:], in0=tanh[t, Z_HALF][:], in1=fed_back[t][:], op=ALU.add)
@@ -147,20 +159,12 @@ def tile_koslmcell_pa_s_kernel(
 
         for t in range(TILES):
             gate(t, M_HALF)
-            m_t = keep.tile([P, H], F32, name="m_t_%d" % t)
-            nc.scalar.mul(out=m_t[:], in_=tanh[t, M_HALF][:], mul=M_SCALE)
-            nc.sync.dma_start(out=by_tile(out_1)[:, t, :], in_=m_t[:])
-            if t > 0:
-                innovate(t - 1)
             gate(t, Z_HALF)
             nc.sync.dma_start(out=by_tile(out_0)[:, t, :], in_=tanh[t, Z_HALF][:])
-            fed_back[t] = keep.tile([P, H], F32, name="fed_back_%d" % t)
-            nc.vector.scalar_tensor_tensor(
-                out=fed_back[t][:],
-                in0=tanh[t, M_HALF][:],
-                scalar=M_SCALE,
-                in1=decay_c[:, t, :],
-                op0=ALU.mult,
-                op1=ALU.mult,
-            )
-        innovate(TILES - 1)
+            if t == 0:
+                feed_back(0, nc.gpsimd)
+                scale_m(0)
+        innovate(0)
+        feed_back(1, nc.vector)
+        scale_m(1)
+        innovate(1)

@@ -1,3 +1,4 @@
+import math
 from contextlib import ExitStack
 
 import concourse.mybir as mybir
@@ -61,27 +62,23 @@ def tile_koslmcell_pa_s_kernel(
         ident = keep.tile([P, P], F32)
         make_identity(nc, ident[:])
 
-        nc.sync.dma_start(out=vec_rows[0:1, 0 : 2 * H], in_=b_ih.unsqueeze(0))
-        nc.sync.dma_start(out=vec_rows[1:2, 0 : 2 * H], in_=b_hh.unsqueeze(0))
-        nc.sync.dma_start(out=vec_rows[2:3, 0:H], in_=z_bias.unsqueeze(0))
-        nc.sync.dma_start(out=vec_rows[2:3, H : 2 * H], in_=m_bias.unsqueeze(0))
         x_sb = keep.tile([P, TILES, K], BF16)
         h_sb = keep.tile([P, TILES, K], BF16)
         nc.scalar.dma_start(out=x_sb[:], in_=by_tile(x))
         nc.scalar.dma_start(out=h_sb[:], in_=by_tile(h_prev))
+        nc.sync.dma_start(out=vec_rows[0:1, 0 : 2 * H], in_=b_ih.unsqueeze(0))
+        nc.sync.dma_start(out=vec_rows[1:2, 0 : 2 * H], in_=b_hh.unsqueeze(0))
+        nc.sync.dma_start(out=vec_rows[2:3, 0:H], in_=z_bias.unsqueeze(0))
+        nc.sync.dma_start(out=vec_rows[2:3, H : 2 * H], in_=m_bias.unsqueeze(0))
 
-        def load_scale_rows(o, scales):
+        w_words = keep.tile([P, 2, 4 * H], U8, align_bytes=64)
+        for o, (words, scales) in enumerate(((W_ih_words, W_ih_scales), (W_hh_words, W_hh_scales))):
+            nc.sync.dma_start(out=w_words[:, o, :].bitcast(I32), in_=words[0].bitcast(I32))
             for q in range(4):
                 nc.sync.dma_start(
                     out=w_planes[32 * q : 32 * q + 4, o, :].bitcast(I32),
                     in_=scales[0, 4 * q : 4 * q + 4, :].bitcast(I32),
                 )
-
-        w_words = keep.tile([P, 2, 4 * H], U8, align_bytes=64)
-        load_scale_rows(0, W_ih_scales)
-        nc.sync.dma_start(out=w_words[:, 0, :].bitcast(I32), in_=W_ih_words[0].bitcast(I32))
-        nc.sync.dma_start(out=w_words[:, 1, :].bitcast(I32), in_=W_hh_words[0].bitcast(I32))
-        load_scale_rows(1, W_hh_scales)
         nc.gpsimd.dma_start(out=vec_rows[0:1, 2 * H : 3 * H], in_=log_lambda.unsqueeze(0))
         c_sb = keep.tile([P, TILES, H], BF16)
         nc.gpsimd.dma_start(out=c_sb[:], in_=by_tile(c_prev))
@@ -108,12 +105,11 @@ def tile_koslmcell_pa_s_kernel(
         lam_ps = psum.tile([P, H], F32, tag="bank")
         nc.tensor.matmul(out=lam_ps[:], lhsT=ones[:], rhs=vec_rows[:, 2 * H : 3 * H], start=True, stop=True)
         lam = keep.tile([P, H], F32)
-        nc.scalar.activation(out=lam[:], in_=lam_ps[:], func=ACT.Exp)
+        nc.scalar.activation(out=lam[:], in_=lam_ps[:], func=ACT.Exp, bias=math.log(M_SCALE))
+        product_engine = (nc.gpsimd, nc.vector)
         decay_c = keep.tile([P, TILES, H], F32)
         for t in range(TILES):
-            nc.vector.scalar_tensor_tensor(
-                out=decay_c[:, t, :], in0=c_sb[:, t, :], scalar=M_SCALE, in1=lam[:], op0=ALU.mult, op1=ALU.mult
-            )
+            product_engine[t].tensor_tensor(out=decay_c[:, t, :], in0=c_sb[:, t, :], in1=lam[:], op=ALU.mult)
 
         bias = keep.tile([P, 2, H], F32)
         for half in (M_HALF, Z_HALF):
@@ -148,9 +144,11 @@ def tile_koslmcell_pa_s_kernel(
             nc.scalar.mul(out=m_t[:], in_=tanh[t, M_HALF][:], mul=M_SCALE)
             nc.sync.dma_start(out=by_tile(out_1)[:, t, :], in_=m_t[:])
 
-        def feed_back(t, engine):
+        def feed_back(t):
             fed_back[t] = keep.tile([P, H], F32, name="fed_back_%d" % t)
-            engine.tensor_tensor(out=fed_back[t][:], in0=tanh[t, M_HALF][:], in1=decay_c[:, t, :], op=ALU.mult)
+            product_engine[t].tensor_tensor(
+                out=fed_back[t][:], in0=tanh[t, M_HALF][:], in1=decay_c[:, t, :], op=ALU.mult
+            )
 
         def innovate(t):
             innov = keep.tile([P, H], F32, name="innov_%d" % t)
@@ -162,9 +160,9 @@ def tile_koslmcell_pa_s_kernel(
             gate(t, Z_HALF)
             nc.sync.dma_start(out=by_tile(out_0)[:, t, :], in_=tanh[t, Z_HALF][:])
             if t == 0:
-                feed_back(0, nc.gpsimd)
+                feed_back(0)
                 scale_m(0)
         innovate(0)
-        feed_back(1, nc.vector)
+        feed_back(1)
         scale_m(1)
         innovate(1)

@@ -54,9 +54,10 @@ def tile_koslmcell_pa_s_kernel(
         stack.enter_context(tc.manual_schedule())
 
         vec_rows = keep.tile([P, 3 * H], BF16)
-        nc.vector.memset(vec_rows[:], 0.0)
+        nc.vector.memset(vec_rows[:, 0 : 2 * H].bitcast(I32), 0)
         w_planes = keep.tile([P, 2, 2 * H], U8, align_bytes=64)
         nc.vector.memset(w_planes[:].rearrange("p o n -> p (o n)").bitcast(I32), 0)
+        nc.vector.memset(vec_rows[:, 2 * H : 3 * H].bitcast(I32), 0)
         ones = keep.tile([P, P], BF16)
         nc.vector.memset(ones[:], 1.0)
         ident = keep.tile([P, P], F32)
@@ -89,7 +90,8 @@ def tile_koslmcell_pa_s_kernel(
         grouped = keep.tile([P, 2, TILES, P, 4], BF16, align_bytes=64)
         act_codes = keep.tile([P, 2, TILES, P], U32, align_bytes=64)
         act_planes = keep.tile([P, 2, TILES, P], U8, align_bytes=64)
-        for o, act_sb in enumerate((x_sb, h_sb)):
+
+        def flip_and_quantise(o, act_sb):
             for t in range(TILES):
                 flipped = psum.tile([P, 2, P], F32, tag="bank", name="flipped_%d_%d" % (o, t))
                 for u in range(2):
@@ -102,14 +104,7 @@ def tile_koslmcell_pa_s_kernel(
                     in_=grouped[:, o, t, :, :].rearrange("p r j -> p (r j)"),
                 )
 
-        lam_ps = psum.tile([P, H], F32, tag="bank")
-        nc.tensor.matmul(out=lam_ps[:], lhsT=ones[:], rhs=vec_rows[:, 2 * H : 3 * H], start=True, stop=True)
-        lam = keep.tile([P, H], F32)
-        nc.scalar.activation(out=lam[:], in_=lam_ps[:], func=ACT.Exp, bias=math.log(M_SCALE))
-        product_engine = (nc.gpsimd, nc.vector)
-        decay_c = keep.tile([P, TILES, H], F32)
-        for t in range(TILES):
-            product_engine[t].tensor_tensor(out=decay_c[:, t, :], in0=c_sb[:, t, :], in1=lam[:], op=ALU.mult)
+        flip_and_quantise(0, x_sb)
 
         bias = keep.tile([P, 2, H], F32)
         for half in (M_HALF, Z_HALF):
@@ -118,6 +113,17 @@ def tile_koslmcell_pa_s_kernel(
                 out=bias_ps[:], lhsT=ones[:], rhs=vec_rows[:, H * half : H * (half + 1)], start=True, stop=True
             )
             nc.scalar.copy(out=bias[:, half, :], in_=bias_ps[:])
+
+        flip_and_quantise(1, h_sb)
+
+        lam_ps = psum.tile([P, H], F32, tag="bank")
+        nc.tensor.matmul(out=lam_ps[:], lhsT=ones[:], rhs=vec_rows[:, 2 * H : 3 * H], start=True, stop=True)
+        lam = keep.tile([P, H], F32)
+        nc.scalar.activation(out=lam[:], in_=lam_ps[:], func=ACT.Exp, bias=math.log(M_SCALE))
+        product_engine = (nc.gpsimd, nc.vector)
+        decay_c = keep.tile([P, TILES, H], F32)
+        for t in range(TILES):
+            product_engine[t].tensor_tensor(out=decay_c[:, t, :], in0=c_sb[:, t, :], in1=lam[:], op=ALU.mult)
 
         tanh = {}
         fed_back = {}

@@ -128,18 +128,24 @@ def tile_koslmcell_pa_s_kernel(
         tanh = {}
         fed_back = {}
 
-        def gate(t, half):
-            gates = psum.tile([P, H], F32, tag="bank", name="gates_%d_%d" % (t, half))
+        def products(t):
+            gates = {}
+            for half in (M_HALF, Z_HALF):
+                gates[half] = psum.tile([P, H], F32, tag="bank", name="gates_%d_%d" % (t, half))
             for o in range(2):
-                nc.tensor.matmul_mx(
-                    out=gates[:],
-                    lhsT=act_codes[:, o, t, :].bitcast(FP8X4),
-                    lhsT_scale=act_planes[:, o, t, :],
-                    rhs=w_words[:, o, 2 * H * half : 2 * H * (half + 1)].bitcast(FP4X4),
-                    rhs_scale=w_planes[:, o, H * half : H * (half + 1)],
-                    start=(o == 0),
-                    stop=(o == 1),
-                )
+                for half in (M_HALF, Z_HALF):
+                    nc.tensor.matmul_mx(
+                        out=gates[half][:],
+                        lhsT=act_codes[:, o, t, :].bitcast(FP8X4),
+                        lhsT_scale=act_planes[:, o, t, :],
+                        rhs=w_words[:, o, 2 * H * half : 2 * H * (half + 1)].bitcast(FP4X4),
+                        rhs_scale=w_planes[:, o, H * half : H * (half + 1)],
+                        start=(o == 0),
+                        stop=(o == 1),
+                    )
+            return gates
+
+        def squash(t, half, gates):
             biased = keep.tile([P, H], F32, name="biased_%d_%d" % (t, half))
             nc.vector.tensor_tensor(out=biased[:], in0=gates[:], in1=bias[:, half, :], op=ALU.add)
             tanh[t, half] = keep.tile([P, H], F32, name="tanh_%d_%d" % (t, half))
@@ -162,8 +168,9 @@ def tile_koslmcell_pa_s_kernel(
             nc.sync.dma_start(out=by_tile(out_2)[:, t, :], in_=innov[:])
 
         for t in range(TILES):
-            gate(t, M_HALF)
-            gate(t, Z_HALF)
+            gates = products(t)
+            squash(t, M_HALF, gates[M_HALF])
+            squash(t, Z_HALF, gates[Z_HALF])
             nc.sync.dma_start(out=by_tile(out_0)[:, t, :], in_=tanh[t, Z_HALF][:])
             if t == 0:
                 feed_back(0)

@@ -21,6 +21,8 @@ H = 512
 TILES = B // P
 Z_HALF, M_HALF = 0, 1
 M_SCALE = 1.5
+WARM_PASSES = 4
+LAM_PACK = H // P
 
 FLOPS = 2 * B * (2 * H) * (2 * K)
 
@@ -53,11 +55,15 @@ def tile_koslmcell_pa_s_kernel(
         psum = stack.enter_context(tc.psum_pool(name="psum", bufs=8))
         stack.enter_context(tc.manual_schedule())
 
-        vec_rows = keep.tile([P, 3 * H], BF16)
-        nc.vector.memset(vec_rows[:, 0 : 2 * H].bitcast(I32), 0)
+        warm_src = keep.tile([P, P], F32)
+        nc.vector.memset(warm_src[:], 1.0)
+        warm_ps = psum.tile([P, P], F32, tag="bank")
+        for i in range(WARM_PASSES):
+            nc.tensor.matmul(out=warm_ps[:], lhsT=warm_src[:], rhs=warm_src[:], start=True, stop=True)
+        vec_rows = keep.tile([P, 2 * H], BF16)
+        nc.vector.memset(vec_rows[:].bitcast(I32), 0)
         w_planes = keep.tile([P, 2, 2 * H], U8, align_bytes=64)
         nc.vector.memset(w_planes[:].rearrange("p o n -> p (o n)").bitcast(I32), 0)
-        nc.vector.memset(vec_rows[:, 2 * H : 3 * H].bitcast(I32), 0)
         ones = keep.tile([P, P], BF16)
         nc.vector.memset(ones[:], 1.0)
         ident = keep.tile([P, P], F32)
@@ -80,7 +86,8 @@ def tile_koslmcell_pa_s_kernel(
                     out=w_planes[32 * q : 32 * q + 4, o, :].bitcast(I32),
                     in_=scales[0, 4 * q : 4 * q + 4, :].bitcast(I32),
                 )
-        nc.gpsimd.dma_start(out=vec_rows[0:1, 2 * H : 3 * H], in_=log_lambda.unsqueeze(0))
+        ll_col = keep.tile([P, LAM_PACK], BF16)
+        nc.gpsimd.dma_start(out=ll_col[:], in_=log_lambda.rearrange("(p c) -> p c", c=LAM_PACK))
         c_sb = keep.tile([P, TILES, H], BF16)
         nc.gpsimd.dma_start(out=c_sb[:], in_=by_tile(c_prev))
 
@@ -114,12 +121,16 @@ def tile_koslmcell_pa_s_kernel(
             )
             nc.scalar.copy(out=bias[:, half, :], in_=bias_ps[:])
 
+        lam_col = keep.tile([P, LAM_PACK], F32)
+        nc.scalar.activation(out=lam_col[:], in_=ll_col[:], func=ACT.Exp, bias=math.log(M_SCALE))
+
         flip_and_quantise(1, h_sb)
 
-        lam_ps = psum.tile([P, H], F32, tag="bank")
-        nc.tensor.matmul(out=lam_ps[:], lhsT=ones[:], rhs=vec_rows[:, 2 * H : 3 * H], start=True, stop=True)
+        lam_ps = psum.tile([P, LAM_PACK, P], F32, tag="bank")
+        for c in range(LAM_PACK):
+            nc.tensor.transpose(lam_ps[:, c, :], lam_col[:, c : c + 1].to_broadcast([P, P]), ident[:])
         lam = keep.tile([P, H], F32)
-        nc.scalar.activation(out=lam[:], in_=lam_ps[:], func=ACT.Exp, bias=math.log(M_SCALE))
+        nc.scalar.copy(out=lam[:].rearrange("p (n c) -> p n c", c=LAM_PACK), in_=lam_ps[:].rearrange("p c n -> p n c"))
         product_engine = (nc.gpsimd, nc.vector)
         decay_c = keep.tile([P, TILES, H], F32)
         for t in range(TILES):

@@ -133,8 +133,11 @@ def tile_koslmcell_pa_s_kernel(
         nc.scalar.copy(out=lam[:].rearrange("p (n c) -> p n c", c=LAM_PACK), in_=lam_ps[:].rearrange("p c n -> p n c"))
         product_engine = (nc.gpsimd, nc.vector)
         decay_c = keep.tile([P, TILES, H], F32)
-        for t in range(TILES):
+
+        def decay(t):
             product_engine[t].tensor_tensor(out=decay_c[:, t, :], in0=c_sb[:, t, :], in1=lam[:], op=ALU.mult)
+
+        decay(0)
 
         tanh = {}
         fed_back = {}
@@ -186,6 +189,7 @@ def tile_koslmcell_pa_s_kernel(
             if t == 0:
                 feed_back(0)
                 scale_m(0)
+        decay(1)
         innovate(0)
         feed_back(1)
         scale_m(1)

@@ -79,17 +79,26 @@ def tile_koslmcell_pa_s_kernel(
         nc.sync.dma_start(out=vec_rows[2:3, H : 2 * H], in_=m_bias.unsqueeze(0))
 
         w_words = keep.tile([P, 2, 4 * H], U8, align_bytes=64)
-        for o, (words, scales) in enumerate(((W_ih_words, W_ih_scales), (W_hh_words, W_hh_scales))):
+
+        def load_words(o, words):
             nc.sync.dma_start(out=w_words[:, o, :].bitcast(I32), in_=words[0].bitcast(I32))
-            for q in range(4):
+
+        def load_scales(o, scales, quarters):
+            for q in quarters:
                 nc.sync.dma_start(
                     out=w_planes[32 * q : 32 * q + 4, o, :].bitcast(I32),
                     in_=scales[0, 4 * q : 4 * q + 4, :].bitcast(I32),
                 )
+
+        load_words(0, W_ih_words)
+        load_scales(0, W_ih_scales, (0, 1))
+        load_words(1, W_hh_words)
+        load_scales(0, W_ih_scales, (2, 3))
+        load_scales(1, W_hh_scales, (0, 1, 2, 3))
+        c_sb = keep.tile([P, TILES, H], BF16)
+        nc.sync.dma_start(out=c_sb[:], in_=by_tile(c_prev))
         ll_col = keep.tile([P, LAM_PACK], BF16)
         nc.gpsimd.dma_start(out=ll_col[:], in_=log_lambda.rearrange("(p c) -> p c", c=LAM_PACK))
-        c_sb = keep.tile([P, TILES, H], BF16)
-        nc.gpsimd.dma_start(out=c_sb[:], in_=by_tile(c_prev))
 
         table_warm = keep.tile([P, 1], F32)
         nc.scalar.activation(out=table_warm[:], in_=ones[:, 0:1], func=ACT.Tanh)

@@ -121,6 +121,10 @@ def tile_koslmcell_pa_s_kernel(
                 )
 
         flip_and_quantise(0, x_sb)
+        flip_and_quantise(1, h_sb)
+
+        lam_col = keep.tile([P, LAM_PACK], F32)
+        nc.scalar.activation(out=lam_col[:], in_=ll_col[:], func=ACT.Exp, bias=math.log(M_SCALE))
 
         bias = keep.tile([P, 2, H], F32)
         for half in (M_HALF, Z_HALF):
@@ -129,11 +133,6 @@ def tile_koslmcell_pa_s_kernel(
                 out=bias_ps[:], lhsT=ones[:], rhs=vec_rows[:, H * half : H * (half + 1)], start=True, stop=True
             )
             nc.scalar.copy(out=bias[:, half, :], in_=bias_ps[:])
-
-        lam_col = keep.tile([P, LAM_PACK], F32)
-        nc.scalar.activation(out=lam_col[:], in_=ll_col[:], func=ACT.Exp, bias=math.log(M_SCALE))
-
-        flip_and_quantise(1, h_sb)
 
         lam_ps = psum.tile([P, LAM_PACK, P], F32, tag="bank")
         for c in range(LAM_PACK):

@@ -154,8 +154,8 @@ def tile_koslmcell_pa_s_kernel(
             gates = {}
             for half in (M_HALF, Z_HALF):
                 gates[half] = psum.tile([P, H], F32, tag="bank", name="gates_%d_%d" % (t, half))
-            for o in range(2):
-                for half in (M_HALF, Z_HALF):
+            for half in (M_HALF, Z_HALF):
+                for o in range(2):
                     nc.tensor.matmul_mx(
                         out=gates[half][:],
                         lhsT=act_codes[:, o, t, :].bitcast(FP8X4),

@@ -192,13 +192,14 @@ def tile_koslmcell_pa_s_kernel(
         for t in range(TILES):
             gates = products(t)
             squash(t, M_HALF, gates[M_HALF])
+            if t == 1:
+                decay(1)
             squash(t, Z_HALF, gates[Z_HALF])
             nc.sync.dma_start(out=by_tile(out_0)[:, t, :], in_=tanh[t, Z_HALF][:])
             if t == 0:
                 feed_back(0)
                 scale_m(0)
-        decay(1)
-        innovate(0)
         feed_back(1)
         scale_m(1)
+        innovate(0)
         innovate(1)

@@ -21,7 +21,7 @@ H = 512
 TILES = B // P
 Z_HALF, M_HALF = 0, 1
 M_SCALE = 1.5
-WARM_PASSES = 4
+WARM_PASSES = 3
 LAM_PACK = H // P
 
 FLOPS = 2 * B * (2 * H) * (2 * K)
@@ -55,29 +55,23 @@ def tile_koslmcell_pa_s_kernel(
         psum = stack.enter_context(tc.psum_pool(name="psum", bufs=8))
         stack.enter_context(tc.manual_schedule())
 
-        warm_src = keep.tile([P, P], F32)
-        nc.vector.memset(warm_src[:], 1.0)
-        warm_ps = psum.tile([P, P], F32, tag="bank")
-        for i in range(WARM_PASSES):
-            nc.tensor.matmul(out=warm_ps[:], lhsT=warm_src[:], rhs=warm_src[:], start=True, stop=True)
-        vec_rows = keep.tile([P, 2 * H], BF16)
-        nc.vector.memset(vec_rows[:].bitcast(I32), 0)
         w_planes = keep.tile([P, 2, 2 * H], U8, align_bytes=64)
-        nc.vector.memset(w_planes[:].rearrange("p o n -> p (o n)").bitcast(I32), 0)
+        nc.vector.memset(w_planes[:, 0, :].bitcast(I32), 0)
+        vec_rows = keep.tile([P, 2 * H], BF16)
+        for half in (M_HALF, Z_HALF):
+            nc.vector.memset(vec_rows[:, H * half : H * (half + 1)].bitcast(I32), 0)
+        nc.vector.memset(w_planes[:, 1, :].bitcast(I32), 0)
         ones = keep.tile([P, P], BF16)
         nc.vector.memset(ones[:], 1.0)
         ident = keep.tile([P, P], F32)
         make_identity(nc, ident[:])
+        warm_ps = psum.tile([P, P], F32, tag="bank")
+        for i in range(WARM_PASSES):
+            nc.tensor.matmul(out=warm_ps[:], lhsT=ident[:], rhs=ident[:], start=True, stop=True)
 
         x_sb = keep.tile([P, TILES, K], BF16)
         h_sb = keep.tile([P, TILES, K], BF16)
-        nc.scalar.dma_start(out=x_sb[:], in_=by_tile(x))
-        nc.scalar.dma_start(out=h_sb[:], in_=by_tile(h_prev))
-        nc.sync.dma_start(out=vec_rows[0:1, 0 : 2 * H], in_=b_ih.unsqueeze(0))
-        nc.sync.dma_start(out=vec_rows[1:2, 0 : 2 * H], in_=b_hh.unsqueeze(0))
-        nc.sync.dma_start(out=vec_rows[2:3, 0:H], in_=z_bias.unsqueeze(0))
-        nc.sync.dma_start(out=vec_rows[2:3, H : 2 * H], in_=m_bias.unsqueeze(0))
-
+        c_sb = keep.tile([P, TILES, H], BF16)
         w_words = keep.tile([P, 2, 4 * H], U8, align_bytes=64)
 
         def load_words(o, words):
@@ -90,15 +84,19 @@ def tile_koslmcell_pa_s_kernel(
                     in_=scales[0, 4 * q : 4 * q + 4, :].bitcast(I32),
                 )
 
-        load_words(0, W_ih_words)
-        load_scales(0, W_ih_scales, (0, 1))
-        load_words(1, W_hh_words)
-        load_scales(0, W_ih_scales, (2, 3))
-        load_scales(1, W_hh_scales, (0, 1, 2, 3))
-        c_sb = keep.tile([P, TILES, H], BF16)
-        nc.sync.dma_start(out=c_sb[:], in_=by_tile(c_prev))
         ll_col = keep.tile([P, LAM_PACK], BF16)
-        nc.gpsimd.dma_start(out=ll_col[:], in_=log_lambda.rearrange("(p c) -> p c", c=LAM_PACK))
+        nc.sync.dma_start(out=ll_col[:], in_=log_lambda.rearrange("(p c) -> p c", c=LAM_PACK))
+        load_scales(0, W_ih_scales, (0, 1, 2, 3))
+        nc.sync.dma_start(out=vec_rows[2:3, H : 2 * H], in_=m_bias.unsqueeze(0))
+        nc.scalar.dma_start(out=x_sb[:], in_=by_tile(x))
+        nc.scalar.dma_start(out=h_sb[:], in_=by_tile(h_prev))
+        load_words(0, W_ih_words)
+        load_words(1, W_hh_words)
+        nc.sync.dma_start(out=vec_rows[0:1, :], in_=b_ih.unsqueeze(0))
+        nc.sync.dma_start(out=vec_rows[1:2, :], in_=b_hh.unsqueeze(0))
+        load_scales(1, W_hh_scales, (0, 1, 2, 3))
+        nc.sync.dma_start(out=c_sb[:], in_=by_tile(c_prev))
+        nc.gpsimd.dma_start(out=vec_rows[2:3, 0:H], in_=z_bias.unsqueeze(0))
 
         table_warm = keep.tile([P, 1], F32)
         nc.scalar.activation(out=table_warm[:], in_=ones[:, 0:1], func=ACT.Tanh)
@@ -107,69 +105,86 @@ def tile_koslmcell_pa_s_kernel(
         act_codes = keep.tile([P, 2, TILES, P], U32, align_bytes=64)
         act_planes = keep.tile([P, 2, TILES, P], U8, align_bytes=64)
 
-        def flip_and_quantise(o, act_sb):
-            for t in range(TILES):
-                flipped = psum.tile([P, 2, P], F32, tag="bank", name="flipped_%d_%d" % (o, t))
-                for u in range(2):
-                    nc.tensor.transpose(flipped[:, u, :], act_sb[:].bitcast(F32)[:, t, u : K // 2 : 2], ident[:])
-                copy_out = nc.scalar.copy if t == 0 else nc.vector.tensor_copy
-                copy_out(out=grouped[:, o, t, :, :].bitcast(F32), in_=flipped[:].rearrange("p u r -> p r u"))
-                nc.vector.quantize_mx(
-                    out=act_codes[:, o, t, :].bitcast(FP8X4),
-                    scales=act_planes[:, o, t, :],
-                    in_=grouped[:, o, t, :, :].rearrange("p r j -> p (r j)"),
-                )
+        flipped = {}
 
-        flip_and_quantise(0, x_sb)
-        flip_and_quantise(1, h_sb)
+        def group(o, t):
+            copy_out = nc.scalar.copy if t == 0 else nc.vector.tensor_copy
+            copy_out(out=grouped[:, o, t, :, :].bitcast(F32), in_=flipped[o, t][:].rearrange("p u r -> p r u"))
+
+        def flip(o, t, act_sb):
+            flipped[o, t] = psum.tile([P, 2, P], F32, tag="bank", name="flipped_%d_%d" % (o, t))
+            for u in range(2):
+                nc.tensor.transpose(flipped[o, t][:, u, :], act_sb[:].bitcast(F32)[:, t, u : K // 2 : 2], ident[:])
+
+        def quantise(o, t):
+            nc.vector.quantize_mx(
+                out=act_codes[:, o, t, :].bitcast(FP8X4),
+                scales=act_planes[:, o, t, :],
+                in_=grouped[:, o, t, :, :].rearrange("p r j -> p (r j)"),
+            )
 
         lam_col = keep.tile([P, LAM_PACK], F32)
         nc.scalar.activation(out=lam_col[:], in_=ll_col[:], func=ACT.Exp, bias=math.log(M_SCALE))
 
         bias = keep.tile([P, 2, H], F32)
-        for half in (M_HALF, Z_HALF):
+
+        def spread_bias(half):
             bias_ps = psum.tile([P, H], F32, tag="bank", name="bias_ps_%d" % half)
             nc.tensor.matmul(
                 out=bias_ps[:], lhsT=ones[:], rhs=vec_rows[:, H * half : H * (half + 1)], start=True, stop=True
             )
             nc.scalar.copy(out=bias[:, half, :], in_=bias_ps[:])
 
-        lam_ps = psum.tile([P, LAM_PACK, P], F32, tag="bank")
-        for c in range(LAM_PACK):
-            nc.tensor.transpose(lam_ps[:, c, :], lam_col[:, c : c + 1].to_broadcast([P, P]), ident[:])
         lam = keep.tile([P, H], F32)
-        nc.scalar.copy(out=lam[:].rearrange("p (n c) -> p n c", c=LAM_PACK), in_=lam_ps[:].rearrange("p c n -> p n c"))
+
+        def spread_lam():
+            lam_ps = psum.tile([P, LAM_PACK, P], F32, tag="bank")
+            for c in range(LAM_PACK):
+                nc.tensor.transpose(lam_ps[:, c, :], lam_col[:, c : c + 1].to_broadcast([P, P]), ident[:])
+            return lam_ps
+
         product_engine = (nc.gpsimd, nc.vector)
         decay_c = keep.tile([P, TILES, H], F32)
 
         def decay(t):
             product_engine[t].tensor_tensor(out=decay_c[:, t, :], in0=c_sb[:, t, :], in1=lam[:], op=ALU.mult)
 
-        decay(0)
+        for t in range(TILES):
+            flip(0, t, x_sb)
+            group(0, t)
+        for t in range(TILES):
+            quantise(0, t)
+        lam_ps = spread_lam()
+        flip(1, 0, h_sb)
+        group(1, 0)
+        flip(1, 1, h_sb)
+        quantise(1, 0)
+        group(1, 1)
+        quantise(1, 1)
+        nc.scalar.copy(
+            out=lam[:].rearrange("p (n c) -> p n c", c=LAM_PACK), in_=lam_ps[:].rearrange("p c n -> p n c")
+        )
 
+        gates = {}
         tanh = {}
         fed_back = {}
 
-        def products(t):
-            gates = {}
-            for half in (M_HALF, Z_HALF):
-                gates[half] = psum.tile([P, H], F32, tag="bank", name="gates_%d_%d" % (t, half))
-            for half in (M_HALF, Z_HALF):
-                for o in range(2):
-                    nc.tensor.matmul_mx(
-                        out=gates[half][:],
-                        lhsT=act_codes[:, o, t, :].bitcast(FP8X4),
-                        lhsT_scale=act_planes[:, o, t, :],
-                        rhs=w_words[:, o, 2 * H * half : 2 * H * (half + 1)].bitcast(FP4X4),
-                        rhs_scale=w_planes[:, o, H * half : H * (half + 1)],
-                        start=(o == 0),
-                        stop=(o == 1),
-                    )
-            return gates
+        def multiply(o, t, half):
+            if o == 0:
+                gates[t, half] = psum.tile([P, H], F32, tag="bank", name="gates_%d_%d" % (t, half))
+            nc.tensor.matmul_mx(
+                out=gates[t, half][:],
+                lhsT=act_codes[:, o, t, :].bitcast(FP8X4),
+                lhsT_scale=act_planes[:, o, t, :],
+                rhs=w_words[:, o, 2 * H * half : 2 * H * (half + 1)].bitcast(FP4X4),
+                rhs_scale=w_planes[:, o, H * half : H * (half + 1)],
+                start=(o == 0),
+                stop=(o == 1),
+            )
 
-        def squash(t, half, gates):
+        def squash(t, half):
             biased = keep.tile([P, H], F32, name="biased_%d_%d" % (t, half))
-            nc.vector.tensor_tensor(out=biased[:], in0=gates[:], in1=bias[:, half, :], op=ALU.add)
+            nc.vector.tensor_tensor(out=biased[:], in0=gates[t, half][:], in1=bias[:, half, :], op=ALU.add)
             tanh[t, half] = keep.tile([P, H], F32, name="tanh_%d_%d" % (t, half))
             nc.scalar.activation(out=tanh[t, half][:], in_=biased[:], func=ACT.Tanh)
 
@@ -189,17 +204,25 @@ def tile_koslmcell_pa_s_kernel(
             nc.vector.tensor_tensor(out=innov[:], in0=tanh[t, Z_HALF][:], in1=fed_back[t][:], op=ALU.add)
             nc.sync.dma_start(out=by_tile(out_2)[:, t, :], in_=innov[:])
 
+        spread_bias(M_HALF)
+        multiply(0, 0, M_HALF)
+        spread_bias(Z_HALF)
+        multiply(1, 0, M_HALF)
+        squash(0, M_HALF)
+        multiply(0, 1, M_HALF)
+        multiply(1, 1, M_HALF)
+        squash(1, M_HALF)
+        decay(0)
+        feed_back(0)
+        scale_m(0)
         for t in range(TILES):
-            gates = products(t)
-            squash(t, M_HALF, gates[M_HALF])
-            if t == 1:
-                decay(1)
-            squash(t, Z_HALF, gates[Z_HALF])
+            multiply(0, t, Z_HALF)
+            multiply(1, t, Z_HALF)
+            squash(t, Z_HALF)
             nc.sync.dma_start(out=by_tile(out_0)[:, t, :], in_=tanh[t, Z_HALF][:])
             if t == 0:
-                feed_back(0)
-                scale_m(0)
+                decay(1)
+                scale_m(1)
         feed_back(1)
-        scale_m(1)
         innovate(0)
         innovate(1)

@@ -21,8 +21,7 @@ H = 512
 TILES = B // P
 Z_HALF, M_HALF = 0, 1
 M_SCALE = 1.5
-WARM_PASSES = 3
-LAM_PACK = H // P
+PACK = H // P
 
 FLOPS = 2 * B * (2 * H) * (2 * K)
 
@@ -52,27 +51,31 @@ def tile_koslmcell_pa_s_kernel(
 
     with ExitStack() as stack:
         keep = stack.enter_context(tc.tile_pool(name="keep", bufs=1))
-        psum = stack.enter_context(tc.psum_pool(name="psum", bufs=8))
+        psum = stack.enter_context(tc.psum_pool(name="psum", bufs=7))
         stack.enter_context(tc.manual_schedule())
 
         w_planes = keep.tile([P, 2, 2 * H], U8, align_bytes=64)
         nc.vector.memset(w_planes[:, 0, :].bitcast(I32), 0)
         vec_rows = keep.tile([P, 2 * H], BF16)
-        for half in (M_HALF, Z_HALF):
-            nc.vector.memset(vec_rows[:, H * half : H * (half + 1)].bitcast(I32), 0)
+        nc.vector.memset(vec_rows[:].bitcast(I32), 0)
         nc.vector.memset(w_planes[:, 1, :].bitcast(I32), 0)
         ones = keep.tile([P, P], BF16)
         nc.vector.memset(ones[:], 1.0)
         ident = keep.tile([P, P], F32)
         make_identity(nc, ident[:])
-        warm_ps = psum.tile([P, P], F32, tag="bank")
-        for i in range(WARM_PASSES):
-            nc.tensor.matmul(out=warm_ps[:], lhsT=ident[:], rhs=ident[:], start=True, stop=True)
+        warm_ps = psum.tile([P, P], F32, tag="warm", bufs=1)
+
+        def keep_warm(passes):
+            for i in range(passes):
+                nc.tensor.matmul(out=warm_ps[:], lhsT=ident[:], rhs=ident[:], start=True, stop=True)
+
+        keep_warm(3)
 
         x_sb = keep.tile([P, TILES, K], BF16)
         h_sb = keep.tile([P, TILES, K], BF16)
         c_sb = keep.tile([P, TILES, H], BF16)
         w_words = keep.tile([P, 2, 4 * H], U8, align_bytes=64)
+        lam_bf = keep.tile([P, PACK], BF16)
 
         def load_words(o, words):
             nc.sync.dma_start(out=w_words[:, o, :].bitcast(I32), in_=words[0].bitcast(I32))
@@ -84,22 +87,22 @@ def tile_koslmcell_pa_s_kernel(
                     in_=scales[0, 4 * q : 4 * q + 4, :].bitcast(I32),
                 )
 
-        ll_col = keep.tile([P, LAM_PACK], BF16)
-        nc.sync.dma_start(out=ll_col[:], in_=log_lambda.rearrange("(p c) -> p c", c=LAM_PACK))
-        load_scales(0, W_ih_scales, (0, 1, 2, 3))
-        nc.sync.dma_start(out=vec_rows[2:3, H : 2 * H], in_=m_bias.unsqueeze(0))
         nc.scalar.dma_start(out=x_sb[:], in_=by_tile(x))
-        nc.scalar.dma_start(out=h_sb[:], in_=by_tile(h_prev))
-        load_words(0, W_ih_words)
-        load_words(1, W_hh_words)
+        nc.sync.dma_start(out=lam_bf[:], in_=log_lambda.rearrange("(p c) -> p c", c=PACK))
+        nc.sync.dma_start(out=h_sb[:], in_=by_tile(h_prev))
+        load_scales(0, W_ih_scales, (0,))
         nc.sync.dma_start(out=vec_rows[0:1, :], in_=b_ih.unsqueeze(0))
         nc.sync.dma_start(out=vec_rows[1:2, :], in_=b_hh.unsqueeze(0))
+        nc.sync.dma_start(out=vec_rows[2:3, H : 2 * H], in_=m_bias.unsqueeze(0))
+        load_words(0, W_ih_words)
+        load_words(1, W_hh_words)
+        load_scales(0, W_ih_scales, (1, 2, 3))
         load_scales(1, W_hh_scales, (0, 1, 2, 3))
-        nc.sync.dma_start(out=c_sb[:], in_=by_tile(c_prev))
         nc.gpsimd.dma_start(out=vec_rows[2:3, 0:H], in_=z_bias.unsqueeze(0))
+        nc.gpsimd.dma_start(out=c_sb[:], in_=by_tile(c_prev))
 
         table_warm = keep.tile([P, 1], F32)
-        nc.scalar.activation(out=table_warm[:], in_=ones[:, 0:1], func=ACT.Tanh)
+        nc.scalar.activation(out=table_warm[:], in_=ident[:, 0:1], func=ACT.Tanh)
 
         grouped = keep.tile([P, 2, TILES, P, 4], BF16, align_bytes=64)
         act_codes = keep.tile([P, 2, TILES, P], U32, align_bytes=64)
@@ -123,9 +126,6 @@ def tile_koslmcell_pa_s_kernel(
                 in_=grouped[:, o, t, :, :].rearrange("p r j -> p (r j)"),
             )
 
-        lam_col = keep.tile([P, LAM_PACK], F32)
-        nc.scalar.activation(out=lam_col[:], in_=ll_col[:], func=ACT.Exp, bias=math.log(M_SCALE))
-
         bias = keep.tile([P, 2, H], F32)
 
         def spread_bias(half):
@@ -135,13 +135,14 @@ def tile_koslmcell_pa_s_kernel(
             )
             nc.scalar.copy(out=bias[:, half, :], in_=bias_ps[:])
 
+        lam_cols = keep.tile([P, PACK], F32)
         lam = keep.tile([P, H], F32)
 
         def spread_lam():
-            lam_ps = psum.tile([P, LAM_PACK, P], F32, tag="bank")
-            for c in range(LAM_PACK):
-                nc.tensor.transpose(lam_ps[:, c, :], lam_col[:, c : c + 1].to_broadcast([P, P]), ident[:])
-            return lam_ps
+            lam_ps = psum.tile([P, PACK, P], F32, tag="bank")
+            for c in range(PACK):
+                nc.tensor.transpose(lam_ps[:, c, :], lam_cols[:, c : c + 1].to_broadcast([P, P]), ident[:])
+            nc.scalar.copy(out=lam[:].rearrange("p (n c) -> p n c", c=PACK), in_=lam_ps[:].rearrange("p c n -> p n c"))
 
         product_engine = (nc.gpsimd, nc.vector)
         decay_c = keep.tile([P, TILES, H], F32)
@@ -149,23 +150,23 @@ def tile_koslmcell_pa_s_kernel(
         def decay(t):
             product_engine[t].tensor_tensor(out=decay_c[:, t, :], in0=c_sb[:, t, :], in1=lam[:], op=ALU.mult)
 
-        for t in range(TILES):
-            flip(0, t, x_sb)
-            group(0, t)
-        for t in range(TILES):
-            quantise(0, t)
-        lam_ps = spread_lam()
-        flip(1, 0, h_sb)
-        group(1, 0)
-        flip(1, 1, h_sb)
-        quantise(1, 0)
-        group(1, 1)
-        quantise(1, 1)
-        nc.scalar.copy(
-            out=lam[:].rearrange("p (n c) -> p n c", c=LAM_PACK), in_=lam_ps[:].rearrange("p c n -> p n c")
-        )
+        nc.scalar.activation(out=lam_cols[:], in_=lam_bf[:], func=ACT.Exp, bias=math.log(M_SCALE))
+        def bring_in(o, act_sb):
+            for t in range(TILES):
+                flip(o, t, act_sb)
+                group(o, t)
+            for t in range(TILES):
+                quantise(o, t)
+
+        bring_in(0, x_sb)
+        spread_bias(M_HALF)
+        bring_in(1, h_sb)
+        keep_warm(1)
+        spread_lam()
+        spread_bias(Z_HALF)
 
         gates = {}
+        biased = {}
         tanh = {}
         fed_back = {}
 
@@ -182,15 +183,22 @@ def tile_koslmcell_pa_s_kernel(
                 stop=(o == 1),
             )
 
+        def add_bias(t, half):
+            biased[t, half] = keep.tile([P, H], F32, name="biased_%d_%d" % (t, half))
+            nc.vector.tensor_tensor(out=biased[t, half][:], in0=gates[t, half][:], in1=bias[:, half, :], op=ALU.add)
+
         def squash(t, half):
-            biased = keep.tile([P, H], F32, name="biased_%d_%d" % (t, half))
-            nc.vector.tensor_tensor(out=biased[:], in0=gates[t, half][:], in1=bias[:, half, :], op=ALU.add)
             tanh[t, half] = keep.tile([P, H], F32, name="tanh_%d_%d" % (t, half))
-            nc.scalar.activation(out=tanh[t, half][:], in_=biased[:], func=ACT.Tanh)
+            nc.scalar.activation(out=tanh[t, half][:], in_=biased[t, half][:], func=ACT.Tanh)
 
         def scale_m(t):
             m_t = keep.tile([P, H], F32, name="m_t_%d" % t)
-            nc.scalar.mul(out=m_t[:], in_=tanh[t, M_HALF][:], mul=M_SCALE)
+            if t == 0:
+                nc.gpsimd.tensor_scalar(
+                    out=m_t[:], in0=tanh[t, M_HALF][:], scalar1=M_SCALE, scalar2=0.0, op0=ALU.mult, op1=ALU.add
+                )
+            else:
+                nc.scalar.mul(out=m_t[:], in_=tanh[t, M_HALF][:], mul=M_SCALE)
             nc.sync.dma_start(out=by_tile(out_1)[:, t, :], in_=m_t[:])
 
         def feed_back(t):
@@ -204,25 +212,23 @@ def tile_koslmcell_pa_s_kernel(
             nc.vector.tensor_tensor(out=innov[:], in0=tanh[t, Z_HALF][:], in1=fed_back[t][:], op=ALU.add)
             nc.sync.dma_start(out=by_tile(out_2)[:, t, :], in_=innov[:])
 
-        spread_bias(M_HALF)
-        multiply(0, 0, M_HALF)
-        spread_bias(Z_HALF)
-        multiply(1, 0, M_HALF)
-        squash(0, M_HALF)
-        multiply(0, 1, M_HALF)
-        multiply(1, 1, M_HALF)
-        squash(1, M_HALF)
+        def gate(t, half):
+            multiply(0, t, half)
+            multiply(1, t, half)
+            add_bias(t, half)
+            squash(t, half)
+
         decay(0)
-        feed_back(0)
+        gate(0, M_HALF)
+        gate(0, Z_HALF)
+        nc.sync.dma_start(out=by_tile(out_0)[:, 0, :], in_=tanh[0, Z_HALF][:])
         scale_m(0)
-        for t in range(TILES):
-            multiply(0, t, Z_HALF)
-            multiply(1, t, Z_HALF)
-            squash(t, Z_HALF)
-            nc.sync.dma_start(out=by_tile(out_0)[:, t, :], in_=tanh[t, Z_HALF][:])
-            if t == 0:
-                decay(1)
-                scale_m(1)
+        feed_back(0)
+        gate(1, M_HALF)
+        decay(1)
+        gate(1, Z_HALF)
+        nc.sync.dma_start(out=by_tile(out_0)[:, 1, :], in_=tanh[1, Z_HALF][:])
+        scale_m(1)
         feed_back(1)
-        innovate(0)
         innovate(1)
+        innovate(0)

@@ -57,7 +57,8 @@ def tile_koslmcell_pa_s_kernel(
         w_planes = keep.tile([P, 2, 2 * H], U8, align_bytes=64)
         nc.vector.memset(w_planes[:, 0, :].bitcast(I32), 0)
         vec_rows = keep.tile([P, 2 * H], BF16)
-        nc.vector.memset(vec_rows[:].bitcast(I32), 0)
+        for half in (Z_HALF, M_HALF):
+            nc.vector.memset(vec_rows[:, H * half : H * (half + 1)].bitcast(I32), 0)
         nc.vector.memset(w_planes[:, 1, :].bitcast(I32), 0)
         ones = keep.tile([P, P], BF16)
         nc.vector.memset(ones[:], 1.0)
@@ -95,11 +96,12 @@ def tile_koslmcell_pa_s_kernel(
         nc.sync.dma_start(out=vec_rows[1:2, :], in_=b_hh.unsqueeze(0))
         nc.sync.dma_start(out=vec_rows[2:3, H : 2 * H], in_=m_bias.unsqueeze(0))
         load_words(0, W_ih_words)
+        load_scales(0, W_ih_scales, (1,))
         load_words(1, W_hh_words)
-        load_scales(0, W_ih_scales, (1, 2, 3))
+        load_scales(0, W_ih_scales, (2, 3))
         load_scales(1, W_hh_scales, (0, 1, 2, 3))
+        nc.sync.dma_start(out=c_sb[:], in_=by_tile(c_prev))
         nc.gpsimd.dma_start(out=vec_rows[2:3, 0:H], in_=z_bias.unsqueeze(0))
-        nc.gpsimd.dma_start(out=c_sb[:], in_=by_tile(c_prev))
 
         table_warm = keep.tile([P, 1], F32)
         nc.scalar.activation(out=table_warm[:], in_=ident[:, 0:1], func=ACT.Tanh)
@@ -193,12 +195,7 @@ def tile_koslmcell_pa_s_kernel(
 
         def scale_m(t):
             m_t = keep.tile([P, H], F32, name="m_t_%d" % t)
-            if t == 0:
-                nc.gpsimd.tensor_scalar(
-                    out=m_t[:], in0=tanh[t, M_HALF][:], scalar1=M_SCALE, scalar2=0.0, op0=ALU.mult, op1=ALU.add
-                )
-            else:
-                nc.scalar.mul(out=m_t[:], in_=tanh[t, M_HALF][:], mul=M_SCALE)
+            nc.scalar.mul(out=m_t[:], in_=tanh[t, M_HALF][:], mul=M_SCALE)
             nc.sync.dma_start(out=by_tile(out_1)[:, t, :], in_=m_t[:])
 
         def feed_back(t):
@@ -222,13 +219,13 @@ def tile_koslmcell_pa_s_kernel(
         gate(0, M_HALF)
         gate(0, Z_HALF)
         nc.sync.dma_start(out=by_tile(out_0)[:, 0, :], in_=tanh[0, Z_HALF][:])
-        scale_m(0)
         feed_back(0)
         gate(1, M_HALF)
+        scale_m(0)
         decay(1)
         gate(1, Z_HALF)
         nc.sync.dma_start(out=by_tile(out_0)[:, 1, :], in_=tanh[1, Z_HALF][:])
         scale_m(1)
         feed_back(1)
-        innovate(1)
         innovate(0)
+        innovate(1)

@@ -140,17 +140,29 @@ def tile_koslmcell_pa_s_kernel(
         lam_cols = keep.tile([P, PACK], F32)
         lam = keep.tile([P, H], F32)
 
+        def in_order(row):
+            return row.rearrange("p (n c) -> p n c", c=PACK)
+
         def spread_lam():
             lam_ps = psum.tile([P, PACK, P], F32, tag="bank")
             for c in range(PACK):
                 nc.tensor.transpose(lam_ps[:, c, :], lam_cols[:, c : c + 1].to_broadcast([P, P]), ident[:])
-            nc.scalar.copy(out=lam[:].rearrange("p (n c) -> p n c", c=PACK), in_=lam_ps[:].rearrange("p c n -> p n c"))
+            nc.scalar.copy(out=in_order(lam[:]), in_=lam_ps[:].rearrange("p c n -> p n c"))
+            return lam_ps
 
         product_engine = (nc.gpsimd, nc.vector)
         decay_c = keep.tile([P, TILES, H], F32)
 
-        def decay(t):
-            product_engine[t].tensor_tensor(out=decay_c[:, t, :], in0=c_sb[:, t, :], in1=lam[:], op=ALU.mult)
+        def decay_on_gpsimd(t):
+            nc.gpsimd.tensor_tensor(out=decay_c[:, t, :], in0=c_sb[:, t, :], in1=lam[:], op=ALU.mult)
+
+        def decay_on_vector(t, lam_ps):
+            nc.vector.tensor_tensor(
+                out=in_order(decay_c[:, t, :]),
+                in0=in_order(c_sb[:, t, :]),
+                in1=lam_ps[:].rearrange("p c n -> p n c"),
+                op=ALU.mult,
+            )
 
         nc.scalar.activation(out=lam_cols[:], in_=lam_bf[:], func=ACT.Exp, bias=math.log(M_SCALE))
         def bring_in(o, act_sb):
@@ -164,7 +176,7 @@ def tile_koslmcell_pa_s_kernel(
         spread_bias(M_HALF)
         bring_in(1, h_sb)
         keep_warm(1)
-        spread_lam()
+        lam_ps = spread_lam()
         spread_bias(Z_HALF)
 
         gates = {}
@@ -215,14 +227,14 @@ def tile_koslmcell_pa_s_kernel(
             add_bias(t, half)
             squash(t, half)
 
-        decay(0)
+        decay_on_gpsimd(0)
         gate(0, M_HALF)
         gate(0, Z_HALF)
         nc.sync.dma_start(out=by_tile(out_0)[:, 0, :], in_=tanh[0, Z_HALF][:])
         feed_back(0)
         gate(1, M_HALF)
         scale_m(0)
-        decay(1)
+        decay_on_vector(1, lam_ps)
         gate(1, Z_HALF)
         nc.sync.dma_start(out=by_tile(out_0)[:, 1, :], in_=tanh[1, Z_HALF][:])
         scale_m(1)

@@ -150,7 +150,6 @@ def tile_koslmcell_pa_s_kernel(
             nc.scalar.copy(out=in_order(lam[:]), in_=lam_ps[:].rearrange("p c n -> p n c"))
             return lam_ps
 
-        product_engine = (nc.gpsimd, nc.vector)
         decay_c = keep.tile([P, TILES, H], F32)
 
         def decay_on_gpsimd(t):
@@ -205,14 +204,22 @@ def tile_koslmcell_pa_s_kernel(
             tanh[t, half] = keep.tile([P, H], F32, name="tanh_%d_%d" % (t, half))
             nc.scalar.activation(out=tanh[t, half][:], in_=biased[t, half][:], func=ACT.Tanh)
 
+        def store_z(t):
+            nc.sync.dma_start(out=by_tile(out_0)[:, t, :], in_=tanh[t, Z_HALF][:])
+
         def scale_m(t):
             m_t = keep.tile([P, H], F32, name="m_t_%d" % t)
-            nc.scalar.mul(out=m_t[:], in_=tanh[t, M_HALF][:], mul=M_SCALE)
+            if t == 0:
+                nc.gpsimd.tensor_scalar(
+                    out=m_t[:], in0=tanh[t, M_HALF][:], scalar1=M_SCALE, scalar2=0.0, op0=ALU.mult, op1=ALU.add
+                )
+            else:
+                nc.scalar.mul(out=m_t[:], in_=tanh[t, M_HALF][:], mul=M_SCALE)
             nc.sync.dma_start(out=by_tile(out_1)[:, t, :], in_=m_t[:])
 
         def feed_back(t):
             fed_back[t] = keep.tile([P, H], F32, name="fed_back_%d" % t)
-            product_engine[t].tensor_tensor(
+            nc.vector.tensor_tensor(
                 out=fed_back[t][:], in0=tanh[t, M_HALF][:], in1=decay_c[:, t, :], op=ALU.mult
             )
 
@@ -230,14 +237,14 @@ def tile_koslmcell_pa_s_kernel(
         decay_on_gpsimd(0)
         gate(0, M_HALF)
         gate(0, Z_HALF)
-        nc.sync.dma_start(out=by_tile(out_0)[:, 0, :], in_=tanh[0, Z_HALF][:])
-        feed_back(0)
-        gate(1, M_HALF)
+        store_z(0)
         scale_m(0)
-        decay_on_vector(1, lam_ps)
         gate(1, Z_HALF)
-        nc.sync.dma_start(out=by_tile(out_0)[:, 1, :], in_=tanh[1, Z_HALF][:])
+        store_z(1)
+        gate(1, M_HALF)
         scale_m(1)
-        feed_back(1)
-        innovate(0)
-        innovate(1)
+        decay_on_vector(1, lam_ps)
+        for t in range(TILES):
+            feed_back(t)
+        for t in range(TILES):
+            innovate(t)

@@ -88,8 +88,8 @@ def tile_koslmcell_pa_s_kernel(
                     in_=scales[0, 4 * q : 4 * q + 4, :].bitcast(I32),
                 )
 
-        nc.scalar.dma_start(out=x_sb[:], in_=by_tile(x))
         nc.sync.dma_start(out=lam_bf[:], in_=log_lambda.rearrange("(p c) -> p c", c=PACK))
+        nc.sync.dma_start(out=x_sb[:], in_=by_tile(x))
         nc.sync.dma_start(out=h_sb[:], in_=by_tile(h_prev))
         load_scales(0, W_ih_scales, (0,))
         nc.sync.dma_start(out=vec_rows[0:1, :], in_=b_ih.unsqueeze(0))
@@ -164,16 +164,18 @@ def tile_koslmcell_pa_s_kernel(
             )
 
         nc.scalar.activation(out=lam_cols[:], in_=lam_bf[:], func=ACT.Exp, bias=math.log(M_SCALE))
-        def bring_in(o, act_sb):
-            for t in range(TILES):
-                flip(o, t, act_sb)
-                group(o, t)
-            for t in range(TILES):
-                quantise(o, t)
-
-        bring_in(0, x_sb)
+        for t in range(TILES):
+            flip(0, t, x_sb)
+            group(0, t)
+        for t in range(TILES):
+            quantise(0, t)
+        flip(1, 0, h_sb)
+        group(1, 0)
+        quantise(1, 0)
         spread_bias(M_HALF)
-        bring_in(1, h_sb)
+        flip(1, 1, h_sb)
+        group(1, 1)
+        quantise(1, 1)
         keep_warm(1)
         lam_ps = spread_lam()
         spread_bias(Z_HALF)

import math
from contextlib import ExitStack

import concourse.mybir as mybir
from concourse.masks import make_identity

F32 = mybir.dt.float32
BF16 = mybir.dt.bfloat16
I32 = mybir.dt.int32
U8 = mybir.dt.uint8
U32 = mybir.dt.uint32
FP8X4 = mybir.dt.float8_e4m3fn_x4
FP4X4 = mybir.dt.float4_e2m1fn_x4
ACT = mybir.ActivationFunctionType
ALU = mybir.AluOpType

P = 128
B = 256
K = 512
H = 512
TILES = B // P
Z_HALF, M_HALF = 0, 1
M_SCALE = 1.5
PACK = H // P

FLOPS = 2 * B * (2 * H) * (2 * K)


def tile_koslmcell_pa_s_kernel(
    tc,
    x,
    h_prev,
    c_prev,
    W_ih_words,
    W_ih_scales,
    b_ih,
    W_hh_words,
    W_hh_scales,
    b_hh,
    log_lambda,
    z_bias,
    m_bias,
    out_0,
    out_1,
    out_2,
):
    nc = tc.nc

    def by_tile(dram):
        return dram.rearrange("(p t) j -> p t j", t=TILES)

    with ExitStack() as stack:
        keep = stack.enter_context(tc.tile_pool(name="keep", bufs=1))
        psum = stack.enter_context(tc.psum_pool(name="psum", bufs=7))
        stack.enter_context(tc.manual_schedule())

        w_planes = keep.tile([P, 2, 2 * H], U8, align_bytes=64)
        nc.vector.memset(w_planes[:, 0, :].bitcast(I32), 0)
        vec_rows = keep.tile([P, 2 * H], BF16)
        for half in (Z_HALF, M_HALF):
            nc.vector.memset(vec_rows[:, H * half : H * (half + 1)].bitcast(I32), 0)
        nc.vector.memset(w_planes[:, 1, :].bitcast(I32), 0)
        ones = keep.tile([P, P], BF16)
        nc.vector.memset(ones[:], 1.0)
        ident = keep.tile([P, P], F32)
        make_identity(nc, ident[:])
        warm_ps = psum.tile([P, P], F32, tag="warm", bufs=1)

        def keep_warm(passes):
            for i in range(passes):
                nc.tensor.matmul(out=warm_ps[:], lhsT=ident[:], rhs=ident[:], start=True, stop=True)

        keep_warm(3)

        x_sb = keep.tile([P, TILES, K], BF16)
        h_sb = keep.tile([P, TILES, K], BF16)
        c_sb = keep.tile([P, TILES, H], BF16)
        w_words = keep.tile([P, 2, 4 * H], U8, align_bytes=64)
        lam_bf = keep.tile([P, PACK], BF16)

        def load_words(o, words):
            nc.sync.dma_start(out=w_words[:, o, :].bitcast(I32), in_=words[0].bitcast(I32))

        def load_scales(o, scales, quarters):
            for q in quarters:
                nc.sync.dma_start(
                    out=w_planes[32 * q : 32 * q + 4, o, :].bitcast(I32),
                    in_=scales[0, 4 * q : 4 * q + 4, :].bitcast(I32),
                )

        nc.sync.dma_start(out=lam_bf[:], in_=log_lambda.rearrange("(p c) -> p c", c=PACK))
        nc.sync.dma_start(out=x_sb[:], in_=by_tile(x))
        nc.sync.dma_start(out=h_sb[:], in_=by_tile(h_prev))
        load_scales(0, W_ih_scales, (0,))
        nc.sync.dma_start(out=vec_rows[0:1, :], in_=b_ih.unsqueeze(0))
        nc.sync.dma_start(out=vec_rows[1:2, :], in_=b_hh.unsqueeze(0))
        nc.sync.dma_start(out=vec_rows[2:3, H : 2 * H], in_=m_bias.unsqueeze(0))
        load_words(0, W_ih_words)
        load_scales(0, W_ih_scales, (1,))
        load_words(1, W_hh_words)
        load_scales(0, W_ih_scales, (2, 3))
        load_scales(1, W_hh_scales, (0, 1, 2, 3))
        nc.sync.dma_start(out=c_sb[:], in_=by_tile(c_prev))
        nc.gpsimd.dma_start(out=vec_rows[2:3, 0:H], in_=z_bias.unsqueeze(0))

        table_warm = keep.tile([P, 1], F32)
        nc.scalar.activation(out=table_warm[:], in_=ident[:, 0:1], func=ACT.Tanh)

        grouped = keep.tile([P, 2, TILES, P, 4], BF16, align_bytes=64)
        act_codes = keep.tile([P, 2, TILES, P], U32, align_bytes=64)
        act_planes = keep.tile([P, 2, TILES, P], U8, align_bytes=64)

        flipped = {}

        def group(o, t):
            copy_out = nc.scalar.copy if t == 0 else nc.vector.tensor_copy
            copy_out(out=grouped[:, o, t, :, :].bitcast(F32), in_=flipped[o, t][:].rearrange("p u r -> p r u"))

        def flip(o, t, act_sb):
            flipped[o, t] = psum.tile([P, 2, P], F32, tag="bank", name="flipped_%d_%d" % (o, t))
            for u in range(2):
                nc.tensor.transpose(flipped[o, t][:, u, :], act_sb[:].bitcast(F32)[:, t, u : K // 2 : 2], ident[:])

        def quantise(o, t):
            nc.vector.quantize_mx(
                out=act_codes[:, o, t, :].bitcast(FP8X4),
                scales=act_planes[:, o, t, :],
                in_=grouped[:, o, t, :, :].rearrange("p r j -> p (r j)"),
            )

        bias = keep.tile([P, 2, H], F32)

        def spread_bias(half):
            bias_ps = psum.tile([P, H], F32, tag="bank", name="bias_ps_%d" % half)
            nc.tensor.matmul(
                out=bias_ps[:], lhsT=ones[:], rhs=vec_rows[:, H * half : H * (half + 1)], start=True, stop=True
            )
            nc.scalar.copy(out=bias[:, half, :], in_=bias_ps[:])

        lam_cols = keep.tile([P, PACK], F32)
        lam = keep.tile([P, H], F32)

        def in_order(row):
            return row.rearrange("p (n c) -> p n c", c=PACK)

        def spread_lam():
            lam_ps = psum.tile([P, PACK, P], F32, tag="bank")
            for c in range(PACK):
                nc.tensor.transpose(lam_ps[:, c, :], lam_cols[:, c : c + 1].to_broadcast([P, P]), ident[:])
            nc.scalar.copy(out=in_order(lam[:]), in_=lam_ps[:].rearrange("p c n -> p n c"))
            return lam_ps

        decay_c = keep.tile([P, TILES, H], F32)

        def decay_on_gpsimd(t):
            nc.gpsimd.tensor_tensor(out=decay_c[:, t, :], in0=c_sb[:, t, :], in1=lam[:], op=ALU.mult)

        def decay_on_vector(t, lam_ps):
            nc.vector.tensor_tensor(
                out=in_order(decay_c[:, t, :]),
                in0=in_order(c_sb[:, t, :]),
                in1=lam_ps[:].rearrange("p c n -> p n c"),
                op=ALU.mult,
            )

        nc.scalar.activation(out=lam_cols[:], in_=lam_bf[:], func=ACT.Exp, bias=math.log(M_SCALE))
        for t in range(TILES):
            flip(0, t, x_sb)
            group(0, t)
        for t in range(TILES):
            quantise(0, t)
        flip(1, 0, h_sb)
        group(1, 0)
        quantise(1, 0)
        spread_bias(M_HALF)
        flip(1, 1, h_sb)
        group(1, 1)
        quantise(1, 1)
        keep_warm(1)
        lam_ps = spread_lam()
        spread_bias(Z_HALF)

        gates = {}
        biased = {}
        tanh = {}
        fed_back = {}

        def multiply(o, t, half):
            if o == 0:
                gates[t, half] = psum.tile([P, H], F32, tag="bank", name="gates_%d_%d" % (t, half))
            nc.tensor.matmul_mx(
                out=gates[t, half][:],
                lhsT=act_codes[:, o, t, :].bitcast(FP8X4),
                lhsT_scale=act_planes[:, o, t, :],
                rhs=w_words[:, o, 2 * H * half : 2 * H * (half + 1)].bitcast(FP4X4),
                rhs_scale=w_planes[:, o, H * half : H * (half + 1)],
                start=(o == 0),
                stop=(o == 1),
            )

        def add_bias(t, half):
            biased[t, half] = keep.tile([P, H], F32, name="biased_%d_%d" % (t, half))
            nc.vector.tensor_tensor(out=biased[t, half][:], in0=gates[t, half][:], in1=bias[:, half, :], op=ALU.add)

        def squash(t, half):
            tanh[t, half] = keep.tile([P, H], F32, name="tanh_%d_%d" % (t, half))
            nc.scalar.activation(out=tanh[t, half][:], in_=biased[t, half][:], func=ACT.Tanh)

        def store_z(t):
            nc.sync.dma_start(out=by_tile(out_0)[:, t, :], in_=tanh[t, Z_HALF][:])

        def scale_m(t):
            m_t = keep.tile([P, H], F32, name="m_t_%d" % t)
            if t == 0:
                nc.gpsimd.tensor_scalar(
                    out=m_t[:], in0=tanh[t, M_HALF][:], scalar1=M_SCALE, scalar2=0.0, op0=ALU.mult, op1=ALU.add
                )
            else:
                nc.scalar.mul(out=m_t[:], in_=tanh[t, M_HALF][:], mul=M_SCALE)
            nc.sync.dma_start(out=by_tile(out_1)[:, t, :], in_=m_t[:])

        def feed_back(t):
            fed_back[t] = keep.tile([P, H], F32, name="fed_back_%d" % t)
            nc.vector.tensor_tensor(
                out=fed_back[t][:], in0=tanh[t, M_HALF][:], in1=decay_c[:, t, :], op=ALU.mult
            )

        def innovate(t):
            innov = keep.tile([P, H], F32, name="innov_%d" % t)
            nc.vector.tensor_tensor(out=innov[:], in0=tanh[t, Z_HALF][:], in1=fed_back[t][:], op=ALU.add)
            nc.sync.dma_start(out=by_tile(out_2)[:, t, :], in_=innov[:])

        def gate(t, half):
            multiply(0, t, half)
            multiply(1, t, half)
            add_bias(t, half)
            squash(t, half)

        decay_on_gpsimd(0)
        gate(0, M_HALF)
        gate(0, Z_HALF)
        store_z(0)
        scale_m(0)
        gate(1, Z_HALF)
        store_z(1)
        gate(1, M_HALF)
        scale_m(1)
        decay_on_vector(1, lam_ps)
        for t in range(TILES):
            feed_back(t)
        for t in range(TILES):
            innovate(t)
